import numpy as np
import ml_dtypes


BF16 = ml_dtypes.bfloat16


def bf(x):
    return np.asarray(x, np.float32).astype(BF16)


def f64(x):
    return np.asarray(x).astype(np.float64)


E2M1 = np.array([0.0, 0.5, 1.0, 1.5, 2.0, 3.0, 4.0, 6.0, -0.0, -0.5, -1.0, -1.5, -2.0, -3.0, -4.0, -6.0])


def pack_weight(w, fmt):
    k, n = w.shape
    w = f64(bf(w)).reshape(k // 32, 32, n)
    amax = np.abs(w).max(1)
    if fmt == "e4m3":
        byte = np.frexp(amax)[1] - 1 + 127 - 7
    else:
        mant, ex = np.frexp(amax / 6.0)
        byte = np.where(mant > 0.5, ex, ex - 1) + 127
    byte = np.clip(np.where(amax > 0, byte, 1), 1, 254)
    scaled = (w * np.exp2(127.0 - byte)[:, None, :]).reshape(k, n).astype(np.float32)
    by_word = np.ascontiguousarray(scaled.reshape(k // 512, 128, 4, n).transpose(0, 1, 3, 2))
    if fmt == "e4m3":
        words = by_word.astype(ml_dtypes.float8_e4m3fn).view(np.uint8)
    else:
        c = by_word.astype(ml_dtypes.float4_e2m1fn).view(np.uint8) & 0xF
        words = c[..., 0::2] | (c[..., 1::2] << 4)
    return np.ascontiguousarray(words), np.ascontiguousarray(byte.astype(np.uint8).reshape(k // 512, 16, n))


def unpack_weight(words, scales, fmt):
    g, p, n, _ = words.shape
    if fmt == "e4m3":
        vals = np.ascontiguousarray(words).view(ml_dtypes.float8_e4m3fn).astype(np.float64)
    else:
        nib = np.empty((g, p, n, 4), np.uint8)
        nib[..., 0::2] = words & 0xF
        nib[..., 1::2] = words >> 4
        vals = E2M1[nib]
    vals = vals * np.repeat(np.exp2(scales.astype(np.float64) - 127.0), 8, axis=1)[..., None]
    return vals.transpose(0, 1, 3, 2).reshape(g * 512, n)

def pack4(w):
    words, scales = pack_weight(w, "e2m1")
    return words.reshape(words.shape[0], 128, -1), scales


def unpack4(words, scales):
    return unpack_weight(words.reshape(words.shape[0], 128, -1, 2), scales, "e2m1")


def kspread(k):
    return np.exp2(np.repeat(np.random.randint(-6, 7, k // 32), 32).astype(np.float64))


B, S, H, HD = 2, 64, 8, 448
D = H * HD
HALF = HD // 2


def apply_rope(t, cos, sin):
    t0 = t[..., 0::2]
    t1 = t[..., 1::2]
    out0 = t0 * cos - t1 * sin
    out1 = t0 * sin + t1 * cos
    return np.stack([out0, out1], axis=-1).reshape(t.shape)


def setup_inputs():
    s = kspread(D)
    phi = np.random.uniform(0.0, 2.0 * np.pi, (S, HALF))
    x = np.random.standard_normal((B, S, D)) * s
    x_words, x_scales = pack4(np.ascontiguousarray(x.reshape(B * S, D).T))
    words, scales = pack4(np.random.standard_normal((D, 3 * D)) / np.sqrt(D) / s[:, None])
    return {"x_words": x_words, "x_scales": x_scales,
            "w_qkv_words": words, "w_qkv_scales": scales,
            "cos": bf(np.cos(phi)), "sin": bf(np.sin(phi))}


def reference(x_words, x_scales, w_qkv_words, w_qkv_scales, cos, sin):
    x = unpack4(x_words, x_scales).T.reshape(B, S, D)
    qkv = x @ unpack4(w_qkv_words, w_qkv_scales)
    qkv = qkv.reshape(B, S, 3, H, HD).transpose(2, 0, 3, 1, 4)
    q, k, v = qkv[0], qkv[1], qkv[2]
    c, sn = f64(cos), f64(sin)
    return apply_rope(q, c, sn), apply_rope(k, c, sn), np.ascontiguousarray(v)

@@ -1,0 +1,235 @@
+from contextlib import ExitStack
+
+import concourse.mybir as mybir
+
+F32 = mybir.dt.float32
+BF16 = mybir.dt.bfloat16
+U8 = mybir.dt.uint8
+I32 = mybir.dt.int32
+FP4X4 = mybir.dt.float4_e2m1fn_x4
+MULT = mybir.AluOpType.mult
+ADD = mybir.AluOpType.add
+COPY = mybir.ActivationFunctionType.Copy
+
+P = 128
+PASSES = 7
+SEQ = 64
+HEADS = 8
+HD = 448
+HALF = HD // 2
+DM = HEADS * HD
+NCOL = 3 * DM
+BANK = 512
+GROUP = 2048
+SLOTS = 4
+BANKS_PER_TENSOR = DM // BANK
+PARTS = ((0, 2), (2, 4), (4, 6), (6, 7))
+
+FLOPS = 2 * P * DM * NCOL
+
+SCALE_FORM = "spread16"
+
+
+def tile_ropeflashattention_pa_kernel(
+    tc, x_words, x_scales, w_qkv_words, w_qkv_scales, cos, sin, out_0, out_1, out_2
+):
+    nc = tc.nc
+    outs = (out_0, out_1, out_2)
+    groups = [(n0, min(GROUP, NCOL - n0)) for n0 in range(0, NCOL, GROUP)]
+    w_scale_rows = w_qkv_scales.flatten_outer_dims()
+
+    with ExitStack() as ctx:
+        keep = ctx.enter_context(tc.tile_pool(name="keep", bufs=1))
+        work = ctx.enter_context(tc.tile_pool(name="work", bufs=3))
+        psum = ctx.enter_context(tc.psum_pool(name="psum", bufs=8))
+        ctx.enter_context(tc.manual_schedule())
+
+        xc = keep.tile([P, PASSES, 2 * P], U8, name="xc", align_bytes=64)
+        xs = keep.tile([P, PASSES, P], U8, name="xs", align_bytes=64)
+        ws_last = keep.tile([P, NCOL], U8, name="ws_last", align_bytes=64)
+        wc = [
+            [
+                keep.tile([P, g1 - g0, 2 * GROUP], U8, name="wc%d_%d" % (s, k), align_bytes=64)
+                for k, (g0, g1) in enumerate(PARTS)
+            ]
+            for s in range(SLOTS)
+        ]
+        ws = [
+            keep.tile([P, PASSES - 1, GROUP], U8, name="ws%d" % s, align_bytes=64)
+            for s in range(SLOTS)
+        ]
+        res = [keep.tile([P, DM], F32, name="res%d" % i) for i in range(2)]
+        cos_sb = keep.tile([P, HALF], BF16, name="cos_sb")
+        sin_sb = keep.tile([P, HALF], BF16, name="sin_sb")
+        cos2 = keep.tile([P, 2 * HD], F32, name="cos2")
+        sin_pos = keep.tile([P, 2 * HALF], F32, name="sin_pos")
+        sin_neg = keep.tile([P, 2 * HALF], F32, name="sin_neg")
+
+        def zero(plane):
+            nc.vector.memset(plane.bitcast(I32), 0)
+
+        def load_codes(c, k):
+            n0, ncols = groups[c]
+            g0, g1 = PARTS[k]
+            nc.sync.dma_start(
+                out=wc[c % SLOTS][k][:, :, 0 : 2 * ncols].bitcast(I32),
+                in_=w_qkv_words[g0:g1, :, 2 * n0 : 2 * (n0 + ncols)]
+                .rearrange("g p n -> p g n")
+                .bitcast(I32),
+            )
+
+        def load_scales(c):
+            n0, ncols = groups[c]
+            plane = ws[c % SLOTS]
+            for i in range(4):
+                if SCALE_FORM == "spread16":
+                    nc.sync.dma_start(
+                        out=plane[i:P:8, :, 0:ncols].bitcast(I32),
+                        in_=w_scale_rows[i : i + 16 * (PASSES - 1), n0 : n0 + ncols]
+                        .rearrange("(g e) n -> e g n", e=16)
+                        .bitcast(I32),
+                    )
+                else:
+                    nc.sync.dma_start(
+                        out=plane[i:P:32, :, 0:ncols].bitcast(I32),
+                        in_=w_qkv_scales[0 : PASSES - 1, i:16:4, n0 : n0 + ncols]
+                        .rearrange("g q n -> q g n")
+                        .bitcast(I32),
+                    )
+
+        def load_group(c):
+            load_scales(c)
+            for k in range(len(PARTS)):
+                load_codes(c, k)
+
+        for b in range(2):
+            nc.scalar.dma_start(out=cos_sb[b * SEQ : (b + 1) * SEQ, :], in_=cos)
+            nc.scalar.dma_start(out=sin_sb[b * SEQ : (b + 1) * SEQ, :], in_=sin)
+
+        zero(xs[:].rearrange("p g n -> p (g n)"))
+        zero(ws[0][:].rearrange("p g n -> p (g n)"))
+        zero(ws_last[:])
+        for s in range(1, SLOTS):
+            zero(ws[s][:].rearrange("p g n -> p (g n)"))
+
+        nc.sync.dma_start(
+            out=xc[:].bitcast(I32), in_=x_words.rearrange("g p n -> p g n").bitcast(I32)
+        )
+        load_codes(0, 0)
+        for i in range(4):
+            nc.sync.dma_start(
+                out=xs[i:P:32, :, :].bitcast(I32),
+                in_=x_scales[:, i:16:4, :].rearrange("g q n -> q g n").bitcast(I32),
+            )
+        load_scales(0)
+        load_codes(0, 1)
+        load_codes(0, 2)
+        for i in range(4):
+            nc.sync.dma_start(
+                out=ws_last[i:P:32, :].bitcast(I32),
+                in_=w_qkv_scales[PASSES - 1, i:16:4, :].bitcast(I32),
+            )
+        load_codes(0, 3)
+        for c in range(1, SLOTS):
+            load_group(c)
+
+        cos2_v = cos2[:].rearrange("p (r j t) -> p r j t", r=2, t=2)
+        for r in range(2):
+            for t in range(2):
+                nc.scalar.copy(out=cos2_v[:, r, :, t], in_=cos_sb[:])
+            nc.scalar.copy(out=sin_pos[:, r * HALF : (r + 1) * HALF], in_=sin_sb[:])
+            nc.scalar.activation(
+                out=sin_neg[:, r * HALF : (r + 1) * HALF], in_=sin_sb[:], func=COPY, scale=-1.0
+            )
+
+        def matmuls(c, accs):
+            n0, ncols = groups[c]
+            s = c % SLOTS
+            for k, (g0, g1) in enumerate(PARTS):
+                for g in range(g0, g1):
+                    for b, acc in enumerate(accs):
+                        if g < PASSES - 1:
+                            scale = ws[s][:, g, b * BANK : (b + 1) * BANK]
+                        else:
+                            scale = ws_last[:, n0 + b * BANK : n0 + (b + 1) * BANK]
+                        nc.tensor.matmul_mx(
+                            out=acc[:],
+                            lhsT=xc[:, g, :].bitcast(FP4X4),
+                            lhsT_scale=xs[:, g, :],
+                            rhs=wc[s][k][:, g - g0, 2 * b * BANK : 2 * (b + 1) * BANK].bitcast(FP4X4),
+                            rhs_scale=scale,
+                            start=(g == 0),
+                            stop=(g == PASSES - 1),
+                        )
+
+        def rope_products(acc, jj):
+            pairs = acc[:].rearrange("p (j t) -> p j t", t=2)
+            ra = work.tile([P, BANK], F32, name="ra")
+            rb = work.tile([P, 2, BANK // 2], F32, name="rb")
+            nc.vector.tensor_tensor(
+                out=ra[:], in0=acc[:], in1=cos2[:, 64 * jj : 64 * jj + BANK], op=MULT
+            )
+            nc.vector.tensor_tensor(
+                out=rb[:, 0, :], in0=pairs[:, :, 1],
+                in1=sin_neg[:, 32 * jj : 32 * jj + BANK // 2], op=MULT,
+            )
+            nc.vector.tensor_tensor(
+                out=rb[:, 1, :], in0=pairs[:, :, 0],
+                in1=sin_pos[:, 32 * jj : 32 * jj + BANK // 2], op=MULT,
+            )
+            return ra, rb
+
+        def rope_sum(t, jj, ra, rb):
+            nc.vector.tensor_tensor(
+                out=res[t % 2][:, jj * BANK : (jj + 1) * BANK].rearrange("p (j t) -> p j t", t=2),
+                in0=ra[:].rearrange("p (j t) -> p j t", t=2),
+                in1=rb[:].rearrange("p t j -> p j t"),
+                op=ADD,
+            )
+
+        def store(t, h0, h1, queues):
+            for b in range(2):
+                queues[b].dma_start(
+                    out=outs[t][b, h0:h1, :, :].rearrange("h s d -> s h d"),
+                    in_=res[t % 2][b * SEQ : (b + 1) * SEQ, h0 * HD : h1 * HD].rearrange(
+                        "p (h d) -> p h d", h=h1 - h0
+                    ),
+                )
+
+        def store_after(t, jj):
+            last = t == 2 and jj == BANKS_PER_TENSOR - 1
+            queues = (nc.sync, nc.scalar) if last else (nc.gpsimd, nc.gpsimd)
+            if jj in (1, 3, 5):
+                store(t, jj - 1, jj + 1, queues)
+            elif jj == 6:
+                store(t, 6, 8, queues)
+
+        for c, (n0, ncols) in enumerate(groups):
+            banks = [n0 // BANK + b for b in range(ncols // BANK)]
+            accs = [psum.tile([P, BANK], F32, name="acc") for j in banks]
+            matmuls(c, accs)
+            pending = None
+            for j, acc in zip(banks, accs):
+                t, jj = divmod(j, BANKS_PER_TENSOR)
+                if t < 2:
+                    ra, rb = rope_products(acc, jj)
+                    if pending is not None:
+                        rope_sum(*pending)
+                        store_after(pending[0], pending[1])
+                    pending = (t, jj, ra, rb)
+                else:
+                    if pending is not None:
+                        rope_sum(*pending)
+                        store_after(pending[0], pending[1])
+                        pending = None
+                    dst = res[t % 2][:, jj * BANK : (jj + 1) * BANK]
+                    if jj % 2 == 0:
+                        nc.scalar.copy(out=dst, in_=acc[:])
+                    else:
+                        nc.vector.tensor_copy(out=dst, in_=acc[:])
+                    store_after(t, jj)
+            if pending is not None:
+                rope_sum(*pending)
+                store_after(pending[0], pending[1])
+            if c + SLOTS < len(groups):
+                load_group(c + SLOTS)

@@ -46,6 +46,8 @@ def tile_ropeflashattention_pa_kernel(
 
         xc = keep.tile([P, PASSES, 2 * P], U8, name="xc", align_bytes=64)
         xs = keep.tile([P, PASSES, P], U8, name="xs", align_bytes=64)
+        xc_raw = keep.tile([P, PASSES, 2 * P], U8, name="xc_raw", align_bytes=64)
+        xs_raw = keep.tile([P, PASSES, P], U8, name="xs_raw", align_bytes=64)
         ws_last = keep.tile([P, NCOL], U8, name="ws_last", align_bytes=64)
         wc = [
             [
@@ -103,22 +105,21 @@ def tile_ropeflashattention_pa_kernel(
                 load_codes(c, k)
 
         for b in range(2):
-            nc.scalar.dma_start(out=cos_sb[b * SEQ : (b + 1) * SEQ, :], in_=cos)
-            nc.scalar.dma_start(out=sin_sb[b * SEQ : (b + 1) * SEQ, :], in_=sin)
+            nc.scalar.dma_start(out=cos_sb[b:P:2, :], in_=cos)
+            nc.scalar.dma_start(out=sin_sb[b:P:2, :], in_=sin)
 
-        zero(xs[:].rearrange("p g n -> p (g n)"))
+        zero(xs_raw[:].rearrange("p g n -> p (g n)"))
         zero(ws[0][:].rearrange("p g n -> p (g n)"))
         zero(ws_last[:])
-        for s in range(1, SLOTS):
-            zero(ws[s][:].rearrange("p g n -> p (g n)"))
+        zero(ws[1][:].rearrange("p g n -> p (g n)"))
 
         nc.sync.dma_start(
-            out=xc[:].bitcast(I32), in_=x_words.rearrange("g p n -> p g n").bitcast(I32)
+            out=xc_raw[:].bitcast(I32), in_=x_words.rearrange("g p n -> p g n").bitcast(I32)
         )
         load_codes(0, 0)
         for i in range(4):
             nc.sync.dma_start(
-                out=xs[i:P:32, :, :].bitcast(I32),
+                out=xs_raw[i:P:32, :, :].bitcast(I32),
                 in_=x_scales[:, i:16:4, :].rearrange("g q n -> q g n").bitcast(I32),
             )
         load_scales(0)
@@ -130,7 +131,20 @@ def tile_ropeflashattention_pa_kernel(
                 in_=w_qkv_scales[PASSES - 1, i:16:4, :].bitcast(I32),
             )
         load_codes(0, 3)
-        for c in range(1, SLOTS):
+        load_group(1)
+
+        for b in range(2):
+            nc.vector.tensor_copy(
+                out=xs[:].rearrange("p g (s b) -> p g s b", b=2)[:, :, :, b],
+                in_=xs_raw[:, :, b * SEQ : (b + 1) * SEQ],
+            )
+            nc.vector.tensor_copy(
+                out=xc[:].rearrange("p g (s b w) -> p g s b w", b=2, w=2)[:, :, :, b, :],
+                in_=xc_raw[:, :, 2 * b * SEQ : 2 * (b + 1) * SEQ].rearrange("p g (s w) -> p g s w", w=2),
+            )
+        for s in range(2, SLOTS):
+            zero(ws[s][:].rearrange("p g n -> p (g n)"))
+        for c in range(2, SLOTS):
             load_group(c)
 
         cos2_v = cos2[:].rearrange("p (r j t) -> p r j t", r=2, t=2)
@@ -187,22 +201,21 @@ def tile_ropeflashattention_pa_kernel(
                 op=ADD,
             )
 
-        def store(t, h0, h1, queues):
-            for b in range(2):
-                queues[b].dma_start(
-                    out=outs[t][b, h0:h1, :, :].rearrange("h s d -> s h d"),
-                    in_=res[t % 2][b * SEQ : (b + 1) * SEQ, h0 * HD : h1 * HD].rearrange(
-                        "p (h d) -> p h d", h=h1 - h0
-                    ),
-                )
+        def store(t, h, queue):
+            queue.dma_start(
+                out=outs[t][:, h, :, :].rearrange("b s d -> s b d"),
+                in_=res[t % 2][:, h * HD : (h + 1) * HD],
+            )
 
         def store_after(t, jj):
-            last = t == 2 and jj == BANKS_PER_TENSOR - 1
-            queues = (nc.sync, nc.scalar) if last else (nc.gpsimd, nc.gpsimd)
-            if jj in (1, 3, 5):
-                store(t, jj - 1, jj + 1, queues)
-            elif jj == 6:
-                store(t, 6, 8, queues)
+            if jj < BANKS_PER_TENSOR - 1:
+                store(t, jj, nc.gpsimd)
+            elif t < 2:
+                store(t, 6, nc.gpsimd)
+                store(t, 7, nc.gpsimd)
+            else:
+                store(t, 6, nc.sync)
+                store(t, 7, nc.scalar)
 
         for c, (n0, ncols) in enumerate(groups):
             banks = [n0 // BANK + b for b in range(ncols // BANK)]

@@ -22,6 +22,7 @@ NCOL = 3 * DM
 BANK = 512
 GROUP = 2048
 SLOTS = 4
+AHEAD = 3
 BANKS_PER_TENSOR = DM // BANK
 PARTS = ((0, 2), (2, 4), (4, 6), (6, 7))
 
@@ -144,8 +145,7 @@ def tile_ropeflashattention_pa_kernel(
             )
         for s in range(2, SLOTS):
             zero(ws[s][:].rearrange("p g n -> p (g n)"))
-        for c in range(2, SLOTS):
-            load_group(c)
+        load_group(2)
 
         cos2_v = cos2[:].rearrange("p (r j t) -> p r j t", r=2, t=2)
         for r in range(2):
@@ -209,10 +209,10 @@ def tile_ropeflashattention_pa_kernel(
 
         def store_after(t, jj):
             if jj < BANKS_PER_TENSOR - 1:
-                store(t, jj, nc.gpsimd)
+                store(t, jj, nc.sync)
             elif t < 2:
-                store(t, 6, nc.gpsimd)
-                store(t, 7, nc.gpsimd)
+                store(t, 6, nc.sync)
+                store(t, 7, nc.sync)
             else:
                 store(t, 6, nc.sync)
                 store(t, 7, nc.scalar)
@@ -244,5 +244,5 @@ def tile_ropeflashattention_pa_kernel(
             if pending is not None:
                 rope_sum(*pending)
                 store_after(pending[0], pending[1])
-            if c + SLOTS < len(groups):
-                load_group(c + SLOTS)
+            if c + AHEAD < len(groups):
+                load_group(c + AHEAD)

@@ -28,7 +28,7 @@ PARTS = ((0, 2), (2, 4), (4, 6), (6, 7))
 
 FLOPS = 2 * P * DM * NCOL
 
-SCALE_FORM = "spread16"
+SCALE_FORM = "four"
 
 
 def tile_ropeflashattention_pa_kernel(

@@ -93,11 +93,11 @@ def tile_ropeflashattention_pa_kernel(
                         .bitcast(I32),
                     )
                 else:
-                    nc.sync.dma_start(
-                        out=plane[i:P:32, :, 0:ncols].bitcast(I32),
+                    nc.gpsimd.dma_start(
+                        out=plane[i:P:32, :, 0:ncols].bitcast(F32),
                         in_=w_qkv_scales[0 : PASSES - 1, i:16:4, n0 : n0 + ncols]
                         .rearrange("g q n -> q g n")
-                        .bitcast(I32),
+                        .bitcast(F32),
                     )
 
         def load_group(c):
@@ -127,9 +127,9 @@ def tile_ropeflashattention_pa_kernel(
         load_codes(0, 1)
         load_codes(0, 2)
         for i in range(4):
-            nc.sync.dma_start(
-                out=ws_last[i:P:32, :].bitcast(I32),
-                in_=w_qkv_scales[PASSES - 1, i:16:4, :].bitcast(I32),
+            nc.gpsimd.dma_start(
+                out=ws_last[i:P:32, :].bitcast(F32),
+                in_=w_qkv_scales[PASSES - 1, i:16:4, :].bitcast(F32),
             )
         load_codes(0, 3)
         load_group(1)

@@ -28,8 +28,6 @@ PARTS = ((0, 2), (2, 4), (4, 6), (6, 7))
 
 FLOPS = 2 * P * DM * NCOL
 
-SCALE_FORM = "four"
-
 
 def tile_ropeflashattention_pa_kernel(
     tc, x_words, x_scales, w_qkv_words, w_qkv_scales, cos, sin, out_0, out_1, out_2
@@ -37,11 +35,10 @@ def tile_ropeflashattention_pa_kernel(
     nc = tc.nc
     outs = (out_0, out_1, out_2)
     groups = [(n0, min(GROUP, NCOL - n0)) for n0 in range(0, NCOL, GROUP)]
-    w_scale_rows = w_qkv_scales.flatten_outer_dims()
 
     with ExitStack() as ctx:
         keep = ctx.enter_context(tc.tile_pool(name="keep", bufs=1))
-        work = ctx.enter_context(tc.tile_pool(name="work", bufs=3))
+        work = ctx.enter_context(tc.tile_pool(name="work", bufs=2))
         psum = ctx.enter_context(tc.psum_pool(name="psum", bufs=8))
         ctx.enter_context(tc.manual_schedule())
 
@@ -49,7 +46,6 @@ def tile_ropeflashattention_pa_kernel(
         xs = keep.tile([P, PASSES, P], U8, name="xs", align_bytes=64)
         xc_raw = keep.tile([P, PASSES, 2 * P], U8, name="xc_raw", align_bytes=64)
         xs_raw = keep.tile([P, PASSES, P], U8, name="xs_raw", align_bytes=64)
-        ws_last = keep.tile([P, NCOL], U8, name="ws_last", align_bytes=64)
         wc = [
             [
                 keep.tile([P, g1 - g0, 2 * GROUP], U8, name="wc%d_%d" % (s, k), align_bytes=64)
@@ -58,8 +54,8 @@ def tile_ropeflashattention_pa_kernel(
             for s in range(SLOTS)
         ]
         ws = [
-            keep.tile([P, PASSES - 1, GROUP], U8, name="ws%d" % s, align_bytes=64)
-            for s in range(SLOTS)
+            keep.tile([P, g1 - g0, NCOL], U8, name="ws%d" % k, align_bytes=64)
+            for k, (g0, g1) in enumerate(PARTS)
         ]
         res = [keep.tile([P, DM], F32, name="res%d" % i) for i in range(2)]
         cos_sb = keep.tile([P, HALF], BF16, name="cos_sb")
@@ -81,27 +77,15 @@ def tile_ropeflashattention_pa_kernel(
                 .bitcast(I32),
             )
 
-        def load_scales(c):
-            n0, ncols = groups[c]
-            plane = ws[c % SLOTS]
+        def load_scales(k):
+            g0, g1 = PARTS[k]
             for i in range(4):
-                if SCALE_FORM == "spread16":
-                    nc.sync.dma_start(
-                        out=plane[i:P:8, :, 0:ncols].bitcast(I32),
-                        in_=w_scale_rows[i : i + 16 * (PASSES - 1), n0 : n0 + ncols]
-                        .rearrange("(g e) n -> e g n", e=16)
-                        .bitcast(I32),
-                    )
-                else:
-                    nc.gpsimd.dma_start(
-                        out=plane[i:P:32, :, 0:ncols].bitcast(F32),
-                        in_=w_qkv_scales[0 : PASSES - 1, i:16:4, n0 : n0 + ncols]
-                        .rearrange("g q n -> q g n")
-                        .bitcast(F32),
-                    )
+                nc.gpsimd.dma_start(
+                    out=ws[k][i:P:32, :, :].bitcast(F32),
+                    in_=w_qkv_scales[g0:g1, i:16:4, :].rearrange("g q n -> q g n").bitcast(F32),
+                )
 
         def load_group(c):
-            load_scales(c)
             for k in range(len(PARTS)):
                 load_codes(c, k)
 
@@ -111,7 +95,6 @@ def tile_ropeflashattention_pa_kernel(
 
         zero(xs_raw[:].rearrange("p g n -> p (g n)"))
         zero(ws[0][:].rearrange("p g n -> p (g n)"))
-        zero(ws_last[:])
         zero(ws[1][:].rearrange("p g n -> p (g n)"))
 
         nc.sync.dma_start(
@@ -124,13 +107,9 @@ def tile_ropeflashattention_pa_kernel(
                 in_=x_scales[:, i:16:4, :].rearrange("g q n -> q g n").bitcast(I32),
             )
         load_scales(0)
+        load_scales(1)
         load_codes(0, 1)
         load_codes(0, 2)
-        for i in range(4):
-            nc.gpsimd.dma_start(
-                out=ws_last[i:P:32, :].bitcast(F32),
-                in_=w_qkv_scales[PASSES - 1, i:16:4, :].bitcast(F32),
-            )
         load_codes(0, 3)
         load_group(1)
 
@@ -143,8 +122,9 @@ def tile_ropeflashattention_pa_kernel(
                 out=xc[:].rearrange("p g (s b w) -> p g s b w", b=2, w=2)[:, :, :, b, :],
                 in_=xc_raw[:, :, 2 * b * SEQ : 2 * (b + 1) * SEQ].rearrange("p g (s w) -> p g s w", w=2),
             )
-        for s in range(2, SLOTS):
-            zero(ws[s][:].rearrange("p g n -> p (g n)"))
+        for k in range(2, len(PARTS)):
+            zero(ws[k][:].rearrange("p g n -> p (g n)"))
+            load_scales(k)
         load_group(2)
 
         cos2_v = cos2[:].rearrange("p (r j t) -> p r j t", r=2, t=2)
@@ -162,10 +142,7 @@ def tile_ropeflashattention_pa_kernel(
             for k, (g0, g1) in enumerate(PARTS):
                 for g in range(g0, g1):
                     for b, acc in enumerate(accs):
-                        if g < PASSES - 1:
-                            scale = ws[s][:, g, b * BANK : (b + 1) * BANK]
-                        else:
-                            scale = ws_last[:, n0 + b * BANK : n0 + (b + 1) * BANK]
+                        scale = ws[k][:, g - g0, n0 + b * BANK : n0 + (b + 1) * BANK]
                         nc.tensor.matmul_mx(
                             out=acc[:],
                             lhsT=xc[:, g, :].bitcast(FP4X4),

@@ -79,11 +79,14 @@ def tile_ropeflashattention_pa_kernel(
 
         def load_scales(k):
             g0, g1 = PARTS[k]
-            for i in range(4):
-                nc.gpsimd.dma_start(
-                    out=ws[k][i:P:32, :, :].bitcast(F32),
-                    in_=w_qkv_scales[g0:g1, i:16:4, :].rearrange("g q n -> q g n").bitcast(F32),
-                )
+            for h in range(2):
+                for i in range(4):
+                    nc.sync.dma_start(
+                        out=ws[k][32 * h + i : P : 64, :, :].bitcast(I32),
+                        in_=w_qkv_scales[g0:g1, 4 * h + i : 16 : 8, :]
+                        .rearrange("g q n -> q g n")
+                        .bitcast(I32),
+                    )
 
         def load_group(c):
             for k in range(len(PARTS)):
@@ -97,10 +100,10 @@ def tile_ropeflashattention_pa_kernel(
         zero(ws[0][:].rearrange("p g n -> p (g n)"))
         zero(ws[1][:].rearrange("p g n -> p (g n)"))
 
+        load_codes(0, 0)
         nc.sync.dma_start(
             out=xc_raw[:].bitcast(I32), in_=x_words.rearrange("g p n -> p g n").bitcast(I32)
         )
-        load_codes(0, 0)
         for i in range(4):
             nc.sync.dma_start(
                 out=xs_raw[i:P:32, :, :].bitcast(I32),
@@ -108,10 +111,6 @@ def tile_ropeflashattention_pa_kernel(
             )
         load_scales(0)
         load_scales(1)
-        load_codes(0, 1)
-        load_codes(0, 2)
-        load_codes(0, 3)
-        load_group(1)
 
         for b in range(2):
             nc.vector.tensor_copy(
@@ -125,6 +124,10 @@ def tile_ropeflashattention_pa_kernel(
         for k in range(2, len(PARTS)):
             zero(ws[k][:].rearrange("p g n -> p (g n)"))
             load_scales(k)
+        load_codes(0, 1)
+        load_codes(0, 2)
+        load_codes(0, 3)
+        load_group(1)
         load_group(2)
 
         cos2_v = cos2[:].rearrange("p (r j t) -> p r j t", r=2, t=2)

@@ -21,10 +21,17 @@ DM = HEADS * HD
 NCOL = 3 * DM
 BANK = 512
 GROUP = 2048
-SLOTS = 4
-AHEAD = 3
+RING = 14
+PIECE = 8192
 BANKS_PER_TENSOR = DM // BANK
 PARTS = ((0, 2), (2, 4), (4, 6), (6, 7))
+BY_PASS = tuple([(g, g + 1) for g in range(PASSES)])
+RANGES = (
+    (0, 4096, BY_PASS),
+    (4096, 4096, BY_PASS),
+    (8192, 2048, PARTS),
+    (10240, 512, ((0, 4), (4, 7))),
+)
 
 FLOPS = 2 * P * DM * NCOL
 
@@ -39,6 +46,7 @@ def tile_ropeflashattention_pa_kernel(
     with ExitStack() as ctx:
         keep = ctx.enter_context(tc.tile_pool(name="keep", bufs=1))
         work = ctx.enter_context(tc.tile_pool(name="work", bufs=2))
+        codes = ctx.enter_context(tc.tile_pool(name="codes", bufs=RING))
         psum = ctx.enter_context(tc.psum_pool(name="psum", bufs=8))
         ctx.enter_context(tc.manual_schedule())
 
@@ -46,13 +54,7 @@ def tile_ropeflashattention_pa_kernel(
         xs = keep.tile([P, PASSES, P], U8, name="xs", align_bytes=64)
         xc_raw = keep.tile([P, PASSES, 2 * P], U8, name="xc_raw", align_bytes=64)
         xs_raw = keep.tile([P, PASSES, P], U8, name="xs_raw", align_bytes=64)
-        wc = [
-            [
-                keep.tile([P, g1 - g0, 2 * GROUP], U8, name="wc%d_%d" % (s, k), align_bytes=64)
-                for k, (g0, g1) in enumerate(PARTS)
-            ]
-            for s in range(SLOTS)
-        ]
+        wc = {}
         ws = [
             keep.tile([P, g1 - g0, NCOL], U8, name="ws%d" % k, align_bytes=64)
             for k, (g0, g1) in enumerate(PARTS)
@@ -67,15 +69,19 @@ def tile_ropeflashattention_pa_kernel(
         def zero(plane):
             nc.vector.memset(plane.bitcast(I32), 0)
 
-        def load_codes(c, k):
-            n0, ncols = groups[c]
-            g0, g1 = PARTS[k]
+        def load_codes(r, k):
+            n0, ncols, stretches = RANGES[r]
+            g0, g1 = stretches[k]
+            piece = codes.tile([P, PIECE], U8, name="wc", align_bytes=64)
+            view = piece[:, 0 : 2 * ncols * (g1 - g0)].rearrange("p (g n) -> p g n", g=g1 - g0)
             nc.sync.dma_start(
-                out=wc[c % SLOTS][k][:, :, 0 : 2 * ncols].bitcast(I32),
+                out=view.bitcast(I32),
                 in_=w_qkv_words[g0:g1, :, 2 * n0 : 2 * (n0 + ncols)]
                 .rearrange("g p n -> p g n")
                 .bitcast(I32),
             )
+            for g in range(g0, g1):
+                wc[(r, g)] = view[:, g - g0, :]
 
         def load_scales(k):
             g0, g1 = PARTS[k]
@@ -88,9 +94,6 @@ def tile_ropeflashattention_pa_kernel(
                         .bitcast(I32),
                     )
 
-        def load_group(c):
-            for k in range(len(PARTS)):
-                load_codes(c, k)
 
         for b in range(2):
             nc.scalar.dma_start(out=cos_sb[b:P:2, :], in_=cos)
@@ -124,11 +127,10 @@ def tile_ropeflashattention_pa_kernel(
         for k in range(2, len(PARTS)):
             zero(ws[k][:].rearrange("p g n -> p (g n)"))
             load_scales(k)
-        load_codes(0, 1)
-        load_codes(0, 2)
-        load_codes(0, 3)
-        load_group(1)
-        load_group(2)
+        for k in range(1, 7):
+            load_codes(0, k)
+        for k in range(7):
+            load_codes(1, k)
 
         cos2_v = cos2[:].rearrange("p (r j t) -> p r j t", r=2, t=2)
         for r in range(2):
@@ -141,7 +143,8 @@ def tile_ropeflashattention_pa_kernel(
 
         def matmuls(c, accs):
             n0, ncols = groups[c]
-            s = c % SLOTS
+            r = max([i for i in range(len(RANGES)) if RANGES[i][0] <= n0])
+            off = n0 - RANGES[r][0]
             for k, (g0, g1) in enumerate(PARTS):
                 for g in range(g0, g1):
                     for b, acc in enumerate(accs):
@@ -150,7 +153,7 @@ def tile_ropeflashattention_pa_kernel(
                             out=acc[:],
                             lhsT=xc[:, g, :].bitcast(FP4X4),
                             lhsT_scale=xs[:, g, :],
-                            rhs=wc[s][k][:, g - g0, 2 * b * BANK : 2 * (b + 1) * BANK].bitcast(FP4X4),
+                            rhs=wc[(r, g)][:, 2 * (off + b * BANK) : 2 * (off + (b + 1) * BANK)].bitcast(FP4X4),
                             rhs_scale=scale,
                             start=(g == 0),
                             stop=(g == PASSES - 1),
@@ -201,6 +204,11 @@ def tile_ropeflashattention_pa_kernel(
             banks = [n0 // BANK + b for b in range(ncols // BANK)]
             accs = [psum.tile([P, BANK], F32, name="acc") for j in banks]
             matmuls(c, accs)
+            if c == 1:
+                for k in range(4):
+                    load_codes(2, k)
+                for k in range(2):
+                    load_codes(3, k)
             pending = None
             for j, acc in zip(banks, accs):
                 t, jj = divmod(j, BANKS_PER_TENSOR)
@@ -224,5 +232,3 @@ def tile_ropeflashattention_pa_kernel(
             if pending is not None:
                 rope_sum(*pending)
                 store_after(pending[0], pending[1])
-            if c + AHEAD < len(groups):
-                load_group(c + AHEAD)

@@ -45,7 +45,7 @@ def tile_ropeflashattention_pa_kernel(
 
     with ExitStack() as ctx:
         keep = ctx.enter_context(tc.tile_pool(name="keep", bufs=1))
-        work = ctx.enter_context(tc.tile_pool(name="work", bufs=2))
+        work = ctx.enter_context(tc.tile_pool(name="work", bufs=3))
         codes = ctx.enter_context(tc.tile_pool(name="codes", bufs=RING))
         psum = ctx.enter_context(tc.psum_pool(name="psum", bufs=8))
         ctx.enter_context(tc.manual_schedule())
@@ -62,9 +62,9 @@ def tile_ropeflashattention_pa_kernel(
         res = [keep.tile([P, DM], F32, name="res%d" % i) for i in range(2)]
         cos_sb = keep.tile([P, HALF], BF16, name="cos_sb")
         sin_sb = keep.tile([P, HALF], BF16, name="sin_sb")
-        cos2 = keep.tile([P, 2 * HD], F32, name="cos2")
-        sin_pos = keep.tile([P, 2 * HALF], F32, name="sin_pos")
-        sin_neg = keep.tile([P, 2 * HALF], F32, name="sin_neg")
+        cos2 = keep.tile([P, 2 * HD], BF16, name="cos2")
+        sin_pos = keep.tile([P, 2 * HALF], BF16, name="sin_pos")
+        sin_neg = keep.tile([P, 2 * HALF], BF16, name="sin_neg")
 
         def zero(plane):
             nc.vector.memset(plane.bitcast(I32), 0)
@@ -177,7 +177,7 @@ def tile_ropeflashattention_pa_kernel(
             return ra, rb
 
         def rope_sum(t, jj, ra, rb):
-            nc.vector.tensor_tensor(
+            nc.gpsimd.tensor_tensor(
                 out=res[t % 2][:, jj * BANK : (jj + 1) * BANK].rearrange("p (j t) -> p j t", t=2),
                 in0=ra[:].rearrange("p (j t) -> p j t", t=2),
                 in1=rb[:].rearrange("p t j -> p j t"),
@@ -224,10 +224,7 @@ def tile_ropeflashattention_pa_kernel(
                         store_after(pending[0], pending[1])
                         pending = None
                     dst = res[t % 2][:, jj * BANK : (jj + 1) * BANK]
-                    if jj % 2 == 0:
-                        nc.scalar.copy(out=dst, in_=acc[:])
-                    else:
-                        nc.vector.tensor_copy(out=dst, in_=acc[:])
+                    nc.scalar.copy(out=dst, in_=acc[:])
                     store_after(t, jj)
             if pending is not None:
                 rope_sum(*pending)

@@ -20,8 +20,7 @@ HALF = HD // 2
 DM = HEADS * HD
 NCOL = 3 * DM
 BANK = 512
-GROUP = 2048
-RING = 14
+RING = 12
 PIECE = 8192
 BANKS_PER_TENSOR = DM // BANK
 PARTS = ((0, 2), (2, 4), (4, 6), (6, 7))
@@ -41,11 +40,11 @@ def tile_ropeflashattention_pa_kernel(
 ):
     nc = tc.nc
     outs = (out_0, out_1, out_2)
-    groups = [(n0, min(GROUP, NCOL - n0)) for n0 in range(0, NCOL, GROUP)]
+    pieces = [(r, k) for r in range(len(RANGES)) for k in range(len(RANGES[r][2]))]
 
     with ExitStack() as ctx:
         keep = ctx.enter_context(tc.tile_pool(name="keep", bufs=1))
-        work = ctx.enter_context(tc.tile_pool(name="work", bufs=3))
+        work = ctx.enter_context(tc.tile_pool(name="work", bufs=4))
         codes = ctx.enter_context(tc.tile_pool(name="codes", bufs=RING))
         psum = ctx.enter_context(tc.psum_pool(name="psum", bufs=8))
         ctx.enter_context(tc.manual_schedule())
@@ -59,7 +58,7 @@ def tile_ropeflashattention_pa_kernel(
             keep.tile([P, g1 - g0, NCOL], U8, name="ws%d" % k, align_bytes=64)
             for k, (g0, g1) in enumerate(PARTS)
         ]
-        res = [keep.tile([P, DM], F32, name="res%d" % i) for i in range(2)]
+        res = [keep.tile([P, DM], F32, name="res%d" % i) for i in range(3)]
         cos_sb = keep.tile([P, HALF], BF16, name="cos_sb")
         sin_sb = keep.tile([P, HALF], BF16, name="sin_sb")
         cos2 = keep.tile([P, 2 * HD], BF16, name="cos2")
@@ -94,7 +93,6 @@ def tile_ropeflashattention_pa_kernel(
                         .bitcast(I32),
                     )
 
-
         for b in range(2):
             nc.scalar.dma_start(out=cos_sb[b:P:2, :], in_=cos)
             nc.scalar.dma_start(out=sin_sb[b:P:2, :], in_=sin)
@@ -103,7 +101,7 @@ def tile_ropeflashattention_pa_kernel(
         zero(ws[0][:].rearrange("p g n -> p (g n)"))
         zero(ws[1][:].rearrange("p g n -> p (g n)"))
 
-        load_codes(0, 0)
+        load_codes(*pieces[0])
         nc.sync.dma_start(
             out=xc_raw[:].bitcast(I32), in_=x_words.rearrange("g p n -> p g n").bitcast(I32)
         )
@@ -127,10 +125,8 @@ def tile_ropeflashattention_pa_kernel(
         for k in range(2, len(PARTS)):
             zero(ws[k][:].rearrange("p g n -> p (g n)"))
             load_scales(k)
-        for k in range(1, 7):
-            load_codes(0, k)
-        for k in range(7):
-            load_codes(1, k)
+        for i in range(1, RING):
+            load_codes(*pieces[i])
 
         cos2_v = cos2[:].rearrange("p (r j t) -> p r j t", r=2, t=2)
         for r in range(2):
@@ -141,31 +137,28 @@ def tile_ropeflashattention_pa_kernel(
                 out=sin_neg[:, r * HALF : (r + 1) * HALF], in_=sin_sb[:], func=COPY, scale=-1.0
             )
 
-        def matmuls(c, accs):
-            n0, ncols = groups[c]
-            r = max([i for i in range(len(RANGES)) if RANGES[i][0] <= n0])
-            off = n0 - RANGES[r][0]
-            for k, (g0, g1) in enumerate(PARTS):
-                for g in range(g0, g1):
-                    for b, acc in enumerate(accs):
-                        scale = ws[k][:, g - g0, n0 + b * BANK : n0 + (b + 1) * BANK]
-                        nc.tensor.matmul_mx(
-                            out=acc[:],
-                            lhsT=xc[:, g, :].bitcast(FP4X4),
-                            lhsT_scale=xs[:, g, :],
-                            rhs=wc[(r, g)][:, 2 * (off + b * BANK) : 2 * (off + (b + 1) * BANK)].bitcast(FP4X4),
-                            rhs_scale=scale,
-                            start=(g == 0),
-                            stop=(g == PASSES - 1),
-                        )
+        def part_of(g):
+            return [k for k, (g0, g1) in enumerate(PARTS) if g0 <= g < g1][0]
 
-        def rope_products(acc, jj):
-            pairs = acc[:].rearrange("p (j t) -> p j t", t=2)
-            ra = work.tile([P, BANK], F32, name="ra")
-            rb = work.tile([P, 2, BANK // 2], F32, name="rb")
-            nc.vector.tensor_tensor(
-                out=ra[:], in0=acc[:], in1=cos2[:, 64 * jj : 64 * jj + BANK], op=MULT
+        def matmul(r, g, b, acc):
+            n0 = RANGES[r][0] + b * BANK
+            k = part_of(g)
+            nc.tensor.matmul_mx(
+                out=acc[:],
+                lhsT=xc[:, g, :].bitcast(FP4X4),
+                lhsT_scale=xs[:, g, :],
+                rhs=wc[(r, g)][:, 2 * b * BANK : 2 * (b + 1) * BANK].bitcast(FP4X4),
+                rhs_scale=ws[k][:, g - PARTS[k][0], n0 : n0 + BANK],
+                start=(g == 0),
+                stop=(g == PASSES - 1),
             )
+
+        def bank_of(t, jj):
+            return res[t][:, jj * BANK : (jj + 1) * BANK]
+
+        def rope_sines(t, jj):
+            pairs = bank_of(t, jj).rearrange("p (j t) -> p j t", t=2)
+            rb = work.tile([P, 2, BANK // 2], F32, name="rb")
             nc.vector.tensor_tensor(
                 out=rb[:, 0, :], in0=pairs[:, :, 1],
                 in1=sin_neg[:, 32 * jj : 32 * jj + BANK // 2], op=MULT,
@@ -174,20 +167,21 @@ def tile_ropeflashattention_pa_kernel(
                 out=rb[:, 1, :], in0=pairs[:, :, 0],
                 in1=sin_pos[:, 32 * jj : 32 * jj + BANK // 2], op=MULT,
             )
-            return ra, rb
+            return rb
 
-        def rope_sum(t, jj, ra, rb):
-            nc.gpsimd.tensor_tensor(
-                out=res[t % 2][:, jj * BANK : (jj + 1) * BANK].rearrange("p (j t) -> p j t", t=2),
-                in0=ra[:].rearrange("p (j t) -> p j t", t=2),
-                in1=rb[:].rearrange("p t j -> p j t"),
-                op=ADD,
+        def rope_cosines(t, jj):
+            nc.vector.tensor_tensor(
+                out=bank_of(t, jj), in0=bank_of(t, jj), in1=cos2[:, 64 * jj : 64 * jj + BANK], op=MULT
             )
+
+        def rope_sum(t, jj, rb):
+            pairs = bank_of(t, jj).rearrange("p (j t) -> p j t", t=2)
+            nc.vector.tensor_tensor(out=pairs, in0=pairs, in1=rb[:].rearrange("p t j -> p j t"), op=ADD)
 
         def store(t, h, queue):
             queue.dma_start(
                 out=outs[t][:, h, :, :].rearrange("b s d -> s b d"),
-                in_=res[t % 2][:, h * HD : (h + 1) * HD],
+                in_=res[t][:, h * HD : (h + 1) * HD],
             )
 
         def store_after(t, jj):
@@ -200,32 +194,28 @@ def tile_ropeflashattention_pa_kernel(
                 store(t, 6, nc.sync)
                 store(t, 7, nc.scalar)
 
-        for c, (n0, ncols) in enumerate(groups):
-            banks = [n0 // BANK + b for b in range(ncols // BANK)]
+        loaded = RING
+        for r, (n0, ncols, stretches) in enumerate(RANGES):
+            banks = [divmod(n0 // BANK + b, BANKS_PER_TENSOR) for b in range(ncols // BANK)]
             accs = [psum.tile([P, BANK], F32, name="acc") for j in banks]
-            matmuls(c, accs)
-            if c == 1:
-                for k in range(4):
-                    load_codes(2, k)
-                for k in range(2):
-                    load_codes(3, k)
-            pending = None
-            for j, acc in zip(banks, accs):
-                t, jj = divmod(j, BANKS_PER_TENSOR)
-                if t < 2:
-                    ra, rb = rope_products(acc, jj)
-                    if pending is not None:
-                        rope_sum(*pending)
-                        store_after(pending[0], pending[1])
-                    pending = (t, jj, ra, rb)
-                else:
-                    if pending is not None:
-                        rope_sum(*pending)
-                        store_after(pending[0], pending[1])
-                        pending = None
-                    dst = res[t % 2][:, jj * BANK : (jj + 1) * BANK]
-                    nc.scalar.copy(out=dst, in_=acc[:])
+            for g0, g1 in stretches:
+                for g in range(g0, g1):
+                    for b, acc in enumerate(accs):
+                        matmul(r, g, b, acc)
+                if loaded < len(pieces):
+                    load_codes(*pieces[loaded])
+                    loaded += 1
+            for (t, jj), acc in zip(banks, accs):
+                nc.scalar.copy(out=bank_of(t, jj), in_=acc[:])
+            for t, jj in banks:
+                if t == 2:
                     store_after(t, jj)
-            if pending is not None:
-                rope_sum(*pending)
-                store_after(pending[0], pending[1])
+            turned = [(t, jj) for t, jj in banks if t < 2]
+            for i in range(0, len(turned), 2):
+                two = turned[i : i + 2]
+                rbs = [rope_sines(t, jj) for t, jj in two]
+                for t, jj in two:
+                    rope_cosines(t, jj)
+                for (t, jj), rb in zip(two, rbs):
+                    rope_sum(t, jj, rb)
+                    store_after(t, jj)

@@ -21,6 +21,7 @@ DM = HEADS * HD
 NCOL = 3 * DM
 BANK = 512
 RING = 12
+FRONT = 3
 PIECE = 8192
 BANKS_PER_TENSOR = DM // BANK
 PARTS = ((0, 2), (2, 4), (4, 6), (6, 7))
@@ -98,10 +99,11 @@ def tile_ropeflashattention_pa_kernel(
             nc.scalar.dma_start(out=sin_sb[b:P:2, :], in_=sin)
 
         zero(xs_raw[:].rearrange("p g n -> p (g n)"))
-        zero(ws[0][:].rearrange("p g n -> p (g n)"))
-        zero(ws[1][:].rearrange("p g n -> p (g n)"))
+        for k in range(len(PARTS)):
+            zero(ws[k][:].rearrange("p g n -> p (g n)"))
 
-        load_codes(*pieces[0])
+        for i in range(FRONT):
+            load_codes(*pieces[i])
         nc.sync.dma_start(
             out=xc_raw[:].bitcast(I32), in_=x_words.rearrange("g p n -> p g n").bitcast(I32)
         )
@@ -110,8 +112,8 @@ def tile_ropeflashattention_pa_kernel(
                 out=xs_raw[i:P:32, :, :].bitcast(I32),
                 in_=x_scales[:, i:16:4, :].rearrange("g q n -> q g n").bitcast(I32),
             )
-        load_scales(0)
-        load_scales(1)
+        for k in range(len(PARTS)):
+            load_scales(k)
 
         for b in range(2):
             nc.vector.tensor_copy(
@@ -122,10 +124,7 @@ def tile_ropeflashattention_pa_kernel(
                 out=xc[:].rearrange("p g (s b w) -> p g s b w", b=2, w=2)[:, :, :, b, :],
                 in_=xc_raw[:, :, 2 * b * SEQ : 2 * (b + 1) * SEQ].rearrange("p g (s w) -> p g s w", w=2),
             )
-        for k in range(2, len(PARTS)):
-            zero(ws[k][:].rearrange("p g n -> p (g n)"))
-            load_scales(k)
-        for i in range(1, RING):
+        for i in range(FRONT, RING):
             load_codes(*pieces[i])
 
         cos2_v = cos2[:].rearrange("p (r j t) -> p r j t", r=2, t=2)

@@ -29,8 +29,7 @@ BY_PASS = tuple([(g, g + 1) for g in range(PASSES)])
 RANGES = (
     (0, 4096, BY_PASS),
     (4096, 4096, BY_PASS),
-    (8192, 2048, PARTS),
-    (10240, 512, ((0, 4), (4, 7))),
+    (8192, 2560, BY_PASS),
 )
 
 FLOPS = 2 * P * DM * NCOL

from contextlib import ExitStack

import concourse.mybir as mybir

F32 = mybir.dt.float32
BF16 = mybir.dt.bfloat16
U8 = mybir.dt.uint8
I32 = mybir.dt.int32
FP4X4 = mybir.dt.float4_e2m1fn_x4
MULT = mybir.AluOpType.mult
ADD = mybir.AluOpType.add
COPY = mybir.ActivationFunctionType.Copy

P = 128
PASSES = 7
SEQ = 64
HEADS = 8
HD = 448
HALF = HD // 2
DM = HEADS * HD
NCOL = 3 * DM
BANK = 512
RING = 12
FRONT = 3
PIECE = 8192
BANKS_PER_TENSOR = DM // BANK
PARTS = ((0, 2), (2, 4), (4, 6), (6, 7))
BY_PASS = tuple([(g, g + 1) for g in range(PASSES)])
RANGES = (
    (0, 4096, BY_PASS),
    (4096, 4096, BY_PASS),
    (8192, 2560, BY_PASS),
)

FLOPS = 2 * P * DM * NCOL


def tile_ropeflashattention_pa_kernel(
    tc, x_words, x_scales, w_qkv_words, w_qkv_scales, cos, sin, out_0, out_1, out_2
):
    nc = tc.nc
    outs = (out_0, out_1, out_2)
    pieces = [(r, k) for r in range(len(RANGES)) for k in range(len(RANGES[r][2]))]

    with ExitStack() as ctx:
        keep = ctx.enter_context(tc.tile_pool(name="keep", bufs=1))
        work = ctx.enter_context(tc.tile_pool(name="work", bufs=4))
        codes = ctx.enter_context(tc.tile_pool(name="codes", bufs=RING))
        psum = ctx.enter_context(tc.psum_pool(name="psum", bufs=8))
        ctx.enter_context(tc.manual_schedule())

        xc = keep.tile([P, PASSES, 2 * P], U8, name="xc", align_bytes=64)
        xs = keep.tile([P, PASSES, P], U8, name="xs", align_bytes=64)
        xc_raw = keep.tile([P, PASSES, 2 * P], U8, name="xc_raw", align_bytes=64)
        xs_raw = keep.tile([P, PASSES, P], U8, name="xs_raw", align_bytes=64)
        wc = {}
        ws = [
            keep.tile([P, g1 - g0, NCOL], U8, name="ws%d" % k, align_bytes=64)
            for k, (g0, g1) in enumerate(PARTS)
        ]
        res = [keep.tile([P, DM], F32, name="res%d" % i) for i in range(3)]
        cos_sb = keep.tile([P, HALF], BF16, name="cos_sb")
        sin_sb = keep.tile([P, HALF], BF16, name="sin_sb")
        cos2 = keep.tile([P, 2 * HD], BF16, name="cos2")
        sin_pos = keep.tile([P, 2 * HALF], BF16, name="sin_pos")
        sin_neg = keep.tile([P, 2 * HALF], BF16, name="sin_neg")

        def zero(plane):
            nc.vector.memset(plane.bitcast(I32), 0)

        def load_codes(r, k):
            n0, ncols, stretches = RANGES[r]
            g0, g1 = stretches[k]
            piece = codes.tile([P, PIECE], U8, name="wc", align_bytes=64)
            view = piece[:, 0 : 2 * ncols * (g1 - g0)].rearrange("p (g n) -> p g n", g=g1 - g0)
            nc.sync.dma_start(
                out=view.bitcast(I32),
                in_=w_qkv_words[g0:g1, :, 2 * n0 : 2 * (n0 + ncols)]
                .rearrange("g p n -> p g n")
                .bitcast(I32),
            )
            for g in range(g0, g1):
                wc[(r, g)] = view[:, g - g0, :]

        def load_scales(k):
            g0, g1 = PARTS[k]
            for h in range(2):
                for i in range(4):
                    nc.sync.dma_start(
                        out=ws[k][32 * h + i : P : 64, :, :].bitcast(I32),
                        in_=w_qkv_scales[g0:g1, 4 * h + i : 16 : 8, :]
                        .rearrange("g q n -> q g n")
                        .bitcast(I32),
                    )

        for b in range(2):
            nc.scalar.dma_start(out=cos_sb[b:P:2, :], in_=cos)
            nc.scalar.dma_start(out=sin_sb[b:P:2, :], in_=sin)

        zero(xs_raw[:].rearrange("p g n -> p (g n)"))
        for k in range(len(PARTS)):
            zero(ws[k][:].rearrange("p g n -> p (g n)"))

        for i in range(FRONT):
            load_codes(*pieces[i])
        nc.sync.dma_start(
            out=xc_raw[:].bitcast(I32), in_=x_words.rearrange("g p n -> p g n").bitcast(I32)
        )
        for i in range(4):
            nc.sync.dma_start(
                out=xs_raw[i:P:32, :, :].bitcast(I32),
                in_=x_scales[:, i:16:4, :].rearrange("g q n -> q g n").bitcast(I32),
            )
        for k in range(len(PARTS)):
            load_scales(k)

        for b in range(2):
            nc.vector.tensor_copy(
                out=xs[:].rearrange("p g (s b) -> p g s b", b=2)[:, :, :, b],
                in_=xs_raw[:, :, b * SEQ : (b + 1) * SEQ],
            )
            nc.vector.tensor_copy(
                out=xc[:].rearrange("p g (s b w) -> p g s b w", b=2, w=2)[:, :, :, b, :],
                in_=xc_raw[:, :, 2 * b * SEQ : 2 * (b + 1) * SEQ].rearrange("p g (s w) -> p g s w", w=2),
            )
        for i in range(FRONT, RING):
            load_codes(*pieces[i])

        cos2_v = cos2[:].rearrange("p (r j t) -> p r j t", r=2, t=2)
        for r in range(2):
            for t in range(2):
                nc.scalar.copy(out=cos2_v[:, r, :, t], in_=cos_sb[:])
            nc.scalar.copy(out=sin_pos[:, r * HALF : (r + 1) * HALF], in_=sin_sb[:])
            nc.scalar.activation(
                out=sin_neg[:, r * HALF : (r + 1) * HALF], in_=sin_sb[:], func=COPY, scale=-1.0
            )

        def part_of(g):
            return [k for k, (g0, g1) in enumerate(PARTS) if g0 <= g < g1][0]

        def matmul(r, g, b, acc):
            n0 = RANGES[r][0] + b * BANK
            k = part_of(g)
            nc.tensor.matmul_mx(
                out=acc[:],
                lhsT=xc[:, g, :].bitcast(FP4X4),
                lhsT_scale=xs[:, g, :],
                rhs=wc[(r, g)][:, 2 * b * BANK : 2 * (b + 1) * BANK].bitcast(FP4X4),
                rhs_scale=ws[k][:, g - PARTS[k][0], n0 : n0 + BANK],
                start=(g == 0),
                stop=(g == PASSES - 1),
            )

        def bank_of(t, jj):
            return res[t][:, jj * BANK : (jj + 1) * BANK]

        def rope_sines(t, jj):
            pairs = bank_of(t, jj).rearrange("p (j t) -> p j t", t=2)
            rb = work.tile([P, 2, BANK // 2], F32, name="rb")
            nc.vector.tensor_tensor(
                out=rb[:, 0, :], in0=pairs[:, :, 1],
                in1=sin_neg[:, 32 * jj : 32 * jj + BANK // 2], op=MULT,
            )
            nc.vector.tensor_tensor(
                out=rb[:, 1, :], in0=pairs[:, :, 0],
                in1=sin_pos[:, 32 * jj : 32 * jj + BANK // 2], op=MULT,
            )
            return rb

        def rope_cosines(t, jj):
            nc.vector.tensor_tensor(
                out=bank_of(t, jj), in0=bank_of(t, jj), in1=cos2[:, 64 * jj : 64 * jj + BANK], op=MULT
            )

        def rope_sum(t, jj, rb):
            pairs = bank_of(t, jj).rearrange("p (j t) -> p j t", t=2)
            nc.vector.tensor_tensor(out=pairs, in0=pairs, in1=rb[:].rearrange("p t j -> p j t"), op=ADD)

        def store(t, h, queue):
            queue.dma_start(
                out=outs[t][:, h, :, :].rearrange("b s d -> s b d"),
                in_=res[t][:, h * HD : (h + 1) * HD],
            )

        def store_after(t, jj):
            if jj < BANKS_PER_TENSOR - 1:
                store(t, jj, nc.sync)
            elif t < 2:
                store(t, 6, nc.sync)
                store(t, 7, nc.sync)
            else:
                store(t, 6, nc.sync)
                store(t, 7, nc.scalar)

        loaded = RING
        for r, (n0, ncols, stretches) in enumerate(RANGES):
            banks = [divmod(n0 // BANK + b, BANKS_PER_TENSOR) for b in range(ncols // BANK)]
            accs = [psum.tile([P, BANK], F32, name="acc") for j in banks]
            for g0, g1 in stretches:
                for g in range(g0, g1):
                    for b, acc in enumerate(accs):
                        matmul(r, g, b, acc)
                if loaded < len(pieces):
                    load_codes(*pieces[loaded])
                    loaded += 1
            for (t, jj), acc in zip(banks, accs):
                nc.scalar.copy(out=bank_of(t, jj), in_=acc[:])
            for t, jj in banks:
                if t == 2:
                    store_after(t, jj)
            turned = [(t, jj) for t, jj in banks if t < 2]
            for i in range(0, len(turned), 2):
                two = turned[i : i + 2]
                rbs = [rope_sines(t, jj) for t, jj in two]
                for t, jj in two:
                    rope_cosines(t, jj)
                for (t, jj), rb in zip(two, rbs):
                    rope_sum(t, jj, rb)
                    store_after(t, jj)
